import numpy as np
import ml_dtypes


def mxq(x, axis, fmt="e4m3"):
    dtype, down = {"e4m3": (ml_dtypes.float8_e4m3fn, 7), "e5m2": (ml_dtypes.float8_e5m2, 14)}[fmt]
    v = np.moveaxis(np.asarray(x, np.float32).astype(ml_dtypes.bfloat16).astype(np.float64), axis, -1)
    blocks = v.reshape(v.shape[:-1] + (-1, 32))
    amax = np.abs(blocks).max(-1, keepdims=True)
    byte = np.maximum(np.where(amax > 0, np.frexp(amax)[1] - 1 + 127, 0) - down, 1)
    scale = np.exp2(byte - 127.0)
    codes = (blocks / scale).astype(np.float32).astype(dtype).astype(np.float64)
    return np.moveaxis((codes * scale).reshape(v.shape), -1, axis)


WIDE = False


def mx_kscale(k):
    if not WIDE:
        return np.ones(k)
    levels = np.array([10, -10, 5, -5, 0])
    if k % 512:
        return np.exp2(np.random.permutation(np.resize(levels, k // 32))).repeat(32)
    a = np.empty((k // 512, 16))
    for p in range(k // 512):
        a[p, :8] = np.random.permutation(np.resize(levels, 8))
        for g in range(8):
            far = levels[np.abs(levels - a[p, g]) >= 10]
            a[p, g + 8] = far[np.random.randint(len(far))]
    return np.exp2(a.ravel()).repeat(32)


BF16 = ml_dtypes.bfloat16


def bf(x):
    return np.asarray(x, np.float32).astype(BF16)


def f64(x):
    return np.asarray(x).astype(np.float64)


B, S, D_IN, D_OUT = 2, 256, 2048, 2048


def quant8(w):
    mv = np.max(np.abs(w))
    q = np.ceil(np.log2(mv)) - 6.0
    scale = np.exp2(q)
    return np.round(w / scale) * scale


def setup_inputs():
    s = mx_kscale(D_IN)
    x = np.random.standard_normal((B, S, D_IN))
    weight = np.random.standard_normal((D_OUT, D_IN)) * 3.0 / np.sqrt(D_IN)
    w_upper = quant8(weight)
    w_lower = weight - w_upper
    return {"x": bf(x * s), "weight_upper": bf(w_upper / s[None, :]), "weight_lower": bf(w_lower / s[None, :])}


def core(x, weight_upper, weight_lower):
    xq = mxq(f64(x), 2, "e4m3")
    y_upper = xq @ mxq(f64(weight_upper), 1, "e4m3").T
    y_lower = xq @ mxq(f64(weight_lower), 1, "e4m3").T
    return y_upper + y_lower


def e4m3fn_bytes(y):
    return np.clip(np.asarray(y, np.float64), -448.0, 448.0).astype(np.float32).astype(ml_dtypes.float8_e4m3fn).view(np.uint8)


def reference(x, weight_upper, weight_lower):
    out = core(x, weight_upper, weight_lower)
    s = np.max(np.abs(out), axis=-1, keepdims=True) / 448.0
    return out, e4m3fn_bytes(out / s)

@@ -1,0 +1,245 @@
+from contextlib import ExitStack
+
+import concourse.mybir as mybir
+from concourse.masks import make_identity
+
+F32 = mybir.dt.float32
+BF16 = mybir.dt.bfloat16
+U32 = mybir.dt.uint32
+U8 = mybir.dt.uint8
+FP8X4 = mybir.dt.float8_e4m3fn_x4
+FP8 = mybir.dt.float8_e4m3fn
+ALU = mybir.AluOpType
+ACT = mybir.ActivationFunctionType
+AX = mybir.AxisListType
+
+P = 128
+TOKENS = 512
+K = 2048
+N_OUT = 2048
+FLOPS = 2 * 2 * TOKENS * K * N_OUT
+
+TOKEN_TILES = TOKENS // P
+CHUNK = 512
+CHUNKS = N_OUT // CHUNK
+UNIT_K = 1024
+RAW_UNITS = 6
+TRANSPOSE_BANKS = 5
+SUM_BANKS = 8 - TRANSPOSE_BANKS
+HEAD_UNITS = 3
+WARM_UP = 7
+STEPS_PER_RUN = 3
+LAST_PIECES = ((512,), (512,), (512,), (256, 128, 128))
+MAX_SLOTS = 8
+VECTOR_CAST = 1280
+
+
+def tile_virtual16bmatmul_kernel(tc, x, weight_upper, weight_lower, out_0, out_1):
+    nc = tc.nc
+    x_rows = x.flatten_outer_dims()
+    out_rows = out_0.flatten_outer_dims()
+    byte_rows = out_1.flatten_outer_dims()
+
+    units = []
+    for n in range(CHUNKS):
+        for kh in range(2):
+            if n == 0:
+                units.append((x_rows, 0, kh, -1, False, False))
+            units.append((weight_upper, CHUNK * n, kh, n, kh == 0, False))
+            units.append((weight_lower, CHUNK * n, kh, n, False, kh == 1))
+
+    steps = []
+    for n in range(CHUNKS - 1):
+        chunk_units = [j for j in range(len(units)) if units[j][3] == n]
+        steps.extend((j, i, 0, CHUNK) for j in chunk_units for i in range(SUM_BANKS))
+        steps.extend((j, i, 0, CHUNK) for i in range(SUM_BANKS, TOKEN_TILES) for j in chunk_units)
+    chunk_units = [j for j in range(len(units)) if units[j][3] == CHUNKS - 1]
+    for i in range(TOKEN_TILES):
+        for piece, width in enumerate(LAST_PIECES[i]):
+            steps.extend((j, i, sum(LAST_PIECES[i][:piece]), width) for j in chunk_units)
+
+    with ExitStack() as ctx:
+        const = ctx.enter_context(tc.tile_pool(name="const", bufs=1))
+        raw_pool = ctx.enter_context(tc.tile_pool(name="raw_pool", bufs=2 * RAW_UNITS))
+        split_pool = ctx.enter_context(tc.tile_pool(name="split_pool", bufs=6))
+        grouped_pool = ctx.enter_context(tc.tile_pool(name="grouped_pool", bufs=3))
+        code_pool = ctx.enter_context(tc.tile_pool(name="code_pool", bufs=8))
+        byte_pool = ctx.enter_context(tc.tile_pool(name="byte_pool", bufs=TOKEN_TILES))
+        psum = ctx.enter_context(tc.psum_pool(name="psum", bufs=1))
+        ctx.enter_context(tc.manual_schedule())
+
+        raw_tiles = {}
+        split_tiles = {}
+        codes = {}
+        sums = {}
+        byte_tiles = {}
+        pending_maxima = []
+        maxima_kept = [0] * TOKEN_TILES
+
+        def load(j):
+            src, row0, kh = units[j][:3]
+            for pair in range(2):
+                raw = raw_pool.tile([P, 2, UNIT_K], BF16, name="raw", tag="raw")
+                r0 = row0 + 2 * P * pair
+                nc.sync.dma_start(
+                    out=raw[:],
+                    in_=src[r0 : r0 + 2 * P, UNIT_K * kh : UNIT_K * (kh + 1)].rearrange("(a p) k -> p a k", p=P),
+                )
+                raw_tiles[(j, pair)] = raw
+
+        for j in range(RAW_UNITS):
+            load(j)
+
+        zeros_bf16 = const.tile([P, 512], BF16, name="zeros_bf16")
+        nc.vector.memset(zeros_bf16[:], 0.0)
+        identity = const.tile([P, P], F32, name="identity")
+        make_identity(nc, identity[:])
+        zero = const.tile([P, 1], F32, name="zero")
+        nc.vector.memset(zero[:], 0.0)
+        scratch = const.tile([P, 1], F32, name="scratch")
+        nc.scalar.activation(out=scratch[:], in_=zero[:], func=ACT.Identity, bias=zero[:, 0:1], scale=zero[:, 0:1])
+
+        def idle_matmuls(count):
+            for d in range(count):
+                unused = psum.tile([P, 512], F32, name="unused", tag="sums", bufs=SUM_BANKS)
+                nc.tensor.matmul(out=unused[:], lhsT=zeros_bf16[:, 0:P], rhs=zeros_bf16[:], start=True, stop=True)
+
+        idle_matmuls(WARM_UP)
+
+        x_codes = const.tile([P, 4, TOKENS], U32, name="x_codes", align_bytes=64)
+        x_scales = const.tile([P, 4, TOKENS], U8, name="x_scales", align_bytes=64)
+        rows = []
+        for i in range(TOKEN_TILES):
+            row_tile = const.tile([P, N_OUT + MAX_SLOTS], F32, name="rows%d" % i)
+            rows.append(row_tile)
+        row_max = const.tile([P, TOKEN_TILES], F32, name="row_max")
+        row_inv = const.tile([P, TOKEN_TILES], F32, name="row_inv")
+        row_factor = const.tile([P, TOKEN_TILES], F32, name="row_factor")
+
+        def split_words(j):
+            for pair in range(2):
+                split = split_pool.tile([P, 4, 2, P], F32, name="split", tag="split")
+                nc.vector.tensor_copy(
+                    out=split[:],
+                    in_=raw_tiles[(j, pair)][:]
+                    .rearrange("p a k -> p (a k)")
+                    .bitcast(F32)
+                    .rearrange("p (q m u) -> p q u m", q=4, u=2),
+                )
+                split_tiles[(j, pair)] = split
+
+        def quantize(j, grouped, g):
+            nc.vector.quantize_mx(
+                out=codes[j][0][:, g, :].bitcast(FP8X4),
+                scales=codes[j][1][:, g, :],
+                in_=grouped[:, g, :, :].rearrange("p c t -> p (c t)"),
+            )
+
+        def transpose_and_quantize(j):
+            kh, n = units[j][2:4]
+            grouped = grouped_pool.tile([P, 2, CHUNK, 4], BF16, name="grouped", tag="grouped", align_bytes=64)
+            grouped_words = grouped[:].bitcast(F32)
+            if n < 0:
+                codes[j] = (x_codes[:, 2 * kh : 2 * kh + 2, :], x_scales[:, 2 * kh : 2 * kh + 2, :])
+            else:
+                w_codes = code_pool.tile([P, 2, CHUNK], U32, name="w_codes", tag="w_codes", align_bytes=64)
+                w_scales = code_pool.tile([P, 2, CHUNK], U8, name="w_scales", tag="w_scales", align_bytes=64)
+                codes[j] = (w_codes[:], w_scales[:])
+            head = j < HEAD_UNITS
+            if head:
+                order = [(pair, g) for pair in range(2) for g in range(2)]
+            else:
+                order = [(pair, g) for g in range(2) for pair in range(2)]
+            for b, (pair, g) in enumerate(order):
+                turned = psum.tile([P, 2, 2, P], F32, name="turned", tag="turned", bufs=TRANSPOSE_BANKS)
+                for a in range(2):
+                    for u in range(2):
+                        nc.tensor.transpose(turned[:, a, u, :], split_tiles[(j, pair)][:, 2 * a + g, u, :], identity[:])
+                nc.scalar.copy(
+                    out=grouped_words[:, g, 2 * P * pair : 2 * P * (pair + 1), :].rearrange("p (a r) u -> p a r u", a=2),
+                    in_=turned[:].rearrange("p a u r -> p a r u"),
+                )
+                if head and b == 1:
+                    idle_matmuls(2)
+                if head and b == 3:
+                    idle_matmuls(1)
+                if not head and b == 1:
+                    quantize(j, grouped, 0)
+            if head:
+                quantize(j, grouped, 0)
+            quantize(j, grouped, 1)
+
+        def reduce_pending_maxima():
+            for i, c0, width, slot in pending_maxima:
+                nc.vector.tensor_reduce(
+                    out=rows[i][:, N_OUT + slot : N_OUT + slot + 1], in_=rows[i][:, c0 : c0 + width], axis=AX.X,
+                    op=ALU.max, apply_absolute_value=True,
+                )
+            pending_maxima.clear()
+
+        def scalar_cast_and_store(i):
+            nc.scalar.activation(
+                out=byte_tiles[i][:, VECTOR_CAST:N_OUT], in_=rows[i][:, VECTOR_CAST:N_OUT], func=ACT.Identity,
+                bias=zero[:, 0:1], scale=row_factor[:, i : i + 1], saturate=False,
+            )
+            nc.sync.dma_start(out=byte_rows[P * i : P * (i + 1), :], in_=byte_tiles[i][:].bitcast(U8))
+
+        def multiply(j, i, first_col, width):
+            kh, n, opens, closes = units[j][2:]
+            if opens:
+                bank = psum.tile([P, width], F32, name="bank", tag="sums", bufs=SUM_BANKS)
+                sums[i] = bank
+            for g in range(2):
+                nc.tensor.matmul_mx(
+                    out=sums[i][:],
+                    lhsT=x_codes[:, 2 * kh + g, P * i : P * (i + 1)].bitcast(FP8X4),
+                    lhsT_scale=x_scales[:, 2 * kh + g, P * i : P * (i + 1)],
+                    rhs=codes[j][0][:, g, first_col : first_col + width].bitcast(FP8X4),
+                    rhs_scale=codes[j][1][:, g, first_col : first_col + width],
+                    start=(opens and g == 0),
+                    stop=(closes and g == 1),
+                )
+            if not closes:
+                return
+            c0 = CHUNK * n + first_col
+            nc.scalar.copy(out=rows[i][:, c0 : c0 + width], in_=sums[i][:])
+            nc.sync.dma_start(out=out_rows[P * i : P * (i + 1), c0 : c0 + width], in_=rows[i][:, c0 : c0 + width])
+            if c0 + width < N_OUT:
+                pending_maxima.append((i, c0, width, maxima_kept[i]))
+                maxima_kept[i] += 1
+                return
+            if i > 0:
+                scalar_cast_and_store(i - 1)
+            reduce_pending_maxima()
+            nc.vector.tensor_reduce(
+                out=row_max[:, i : i + 1], in_=rows[i][:, c0 : N_OUT + maxima_kept[i]], axis=AX.X, op=ALU.max,
+                apply_absolute_value=True,
+            )
+            nc.vector.reciprocal(out=row_inv[:, i : i + 1], in_=row_max[:, i : i + 1])
+            nc.vector.tensor_scalar(
+                out=row_factor[:, i : i + 1], in0=row_inv[:, i : i + 1], scalar1=448.0, scalar2=None, op0=ALU.mult
+            )
+            as_bytes = byte_pool.tile([P, N_OUT], FP8, name="as_bytes", tag="as_bytes")
+            byte_tiles[i] = as_bytes
+            nc.vector.tensor_scalar(
+                out=as_bytes[:, 0:VECTOR_CAST], in0=rows[i][:, 0:VECTOR_CAST], scalar1=row_factor[:, i : i + 1],
+                scalar2=None, op0=ALU.mult, saturate=False,
+            )
+
+        done = 0
+        split_words(0)
+        for j in range(len(units)):
+            if j + 1 < len(units):
+                split_words(j + 1)
+            reduce_pending_maxima()
+            transpose_and_quantize(j)
+            if j + RAW_UNITS < len(units):
+                load(j + RAW_UNITS)
+            for s in range(STEPS_PER_RUN):
+                if steps[done][0] < j:
+                    multiply(*steps[done])
+                    done += 1
+        for step in steps[done:]:
+            multiply(*step)
+            reduce_pending_maxima()
+        scalar_cast_and_store(TOKEN_TILES - 1)

@@ -22,16 +22,28 @@ FLOPS = 2 * 2 * TOKENS * K * N_OUT
 TOKEN_TILES = TOKENS // P
 CHUNK = 512
 CHUNKS = N_OUT // CHUNK
-UNIT_K = 1024
-RAW_UNITS = 6
-TRANSPOSE_BANKS = 5
+PASS_K = 512
+PASSES = K // PASS_K
+RAW_TILES = 12
+SMALL_PASSES = 0
+TRANSPOSE_BANKS = 4
 SUM_BANKS = 8 - TRANSPOSE_BANKS
-HEAD_UNITS = 3
+LEAD_TILES = 3
+STAGGER = 0
+DEFER_MAX = 0
 WARM_UP = 7
-STEPS_PER_RUN = 3
-LAST_PIECES = ((512,), (512,), (512,), (256, 128, 128))
+HEAD_IDLE = 1
+DIRECT_BLOCKS = 0
+SPLIT_LEAD = 2
+SPLIT_AFTER = 0
+LAG = 2
+P_SMALL = 3
+P_BIG = 6
+CARRY = 100
+LAST_PIECES = (256, 128, 128)
 MAX_SLOTS = 8
-VECTOR_CAST = 1280
+VECTOR_CAST = 1024
+VECTOR_CAST_LAST = 1024
 
 
 def tile_virtual16bmatmul_kernel(tc, x, weight_upper, weight_lower, out_0, out_1):
@@ -40,30 +52,44 @@ def tile_virtual16bmatmul_kernel(tc, x, weight_upper, weight_lower, out_0, out_1
     out_rows = out_0.flatten_outer_dims()
     byte_rows = out_1.flatten_outer_dims()
 
-    units = []
-    for n in range(CHUNKS):
-        for kh in range(2):
-            if n == 0:
-                units.append((x_rows, 0, kh, -1, False, False))
-            units.append((weight_upper, CHUNK * n, kh, n, kh == 0, False))
-            units.append((weight_lower, CHUNK * n, kh, n, False, kh == 1))
+    blocks = []
+    for g in range(SMALL_PASSES):
+        blocks.append((x_rows, 0, g, 1, -1))
+        blocks.append((weight_upper, 0, g, 1, 0))
+        blocks.append((weight_lower, 0, g, 1, 0))
+    for g in range(SMALL_PASSES, PASSES, 2):
+        blocks.append((x_rows, 0, g, 2, -1))
+        blocks.append((weight_upper, 0, g, 2, 0))
+        blocks.append((weight_lower, 0, g, 2, 0))
+    for n in range(1, CHUNKS):
+        for g in range(0, PASSES, 2):
+            blocks.append((weight_upper, CHUNK * n, g, 2, n))
+            blocks.append((weight_lower, CHUNK * n, g, 2, n))
 
-    steps = []
-    for n in range(CHUNKS - 1):
-        chunk_units = [j for j in range(len(units)) if units[j][3] == n]
-        steps.extend((j, i, 0, CHUNK) for j in chunk_units for i in range(SUM_BANKS))
-        steps.extend((j, i, 0, CHUNK) for i in range(SUM_BANKS, TOKEN_TILES) for j in chunk_units)
-    chunk_units = [j for j in range(len(units)) if units[j][3] == CHUNKS - 1]
-    for i in range(TOKEN_TILES):
-        for piece, width in enumerate(LAST_PIECES[i]):
-            steps.extend((j, i, sum(LAST_PIECES[i][:piece]), width) for j in chunk_units)
+    items = [(b, g) for b in range(len(blocks)) for g in range(blocks[b][3])]
+    first_item = [items.index((b, 0)) for b in range(len(blocks))]
+    runs = [[t for t in range(len(items)) if items[t][0] == b] for b in range(len(blocks))]
+
+    w_items = [t for t in range(len(items)) if blocks[items[t][0]][4] >= 0]
+    per_chunk = len(w_items) // CHUNKS
+    order = []
+    for v in range(len(w_items) + STAGGER * (LEAD_TILES - 1)):
+        for i in range(LEAD_TILES):
+            w = v - STAGGER * i
+            if 0 <= w < len(w_items):
+                order.append((w, i, 0, CHUNK))
+    for i in range(LEAD_TILES, TOKEN_TILES):
+        order.extend((w, i, 0, CHUNK) for w in range(len(w_items) - per_chunk))
+        for piece, width in enumerate(LAST_PIECES):
+            order.extend((w, i, sum(LAST_PIECES[:piece]), width) for w in range(len(w_items) - per_chunk, len(w_items)))
+    steps = [(w_items[w], i, c, width, w % per_chunk == 0, w % per_chunk == per_chunk - 1) for w, i, c, width in order]
 
     with ExitStack() as ctx:
         const = ctx.enter_context(tc.tile_pool(name="const", bufs=1))
-        raw_pool = ctx.enter_context(tc.tile_pool(name="raw_pool", bufs=2 * RAW_UNITS))
+        raw_pool = ctx.enter_context(tc.tile_pool(name="raw_pool", bufs=RAW_TILES))
         split_pool = ctx.enter_context(tc.tile_pool(name="split_pool", bufs=6))
-        grouped_pool = ctx.enter_context(tc.tile_pool(name="grouped_pool", bufs=3))
-        code_pool = ctx.enter_context(tc.tile_pool(name="code_pool", bufs=8))
+        grouped_pool = ctx.enter_context(tc.tile_pool(name="grouped_pool", bufs=6))
+        code_pool = ctx.enter_context(tc.tile_pool(name="code_pool", bufs=32))
         byte_pool = ctx.enter_context(tc.tile_pool(name="byte_pool", bufs=TOKEN_TILES))
         psum = ctx.enter_context(tc.psum_pool(name="psum", bufs=1))
         ctx.enter_context(tc.manual_schedule())
@@ -73,22 +99,47 @@ def tile_virtual16bmatmul_kernel(tc, x, weight_upper, weight_lower, out_0, out_1
         codes = {}
         sums = {}
         byte_tiles = {}
+        released = set()
+        waiting_casts = []
         pending_maxima = []
         maxima_kept = [0] * TOKEN_TILES
+        state = {"loaded": 0, "raw_free": RAW_TILES, "split": 0, "oldest": 0, "done": 0, "credit": 0, "opened": 0, "closed": 0}
 
-        def load(j):
-            src, row0, kh = units[j][:3]
-            for pair in range(2):
-                raw = raw_pool.tile([P, 2, UNIT_K], BF16, name="raw", tag="raw")
-                r0 = row0 + 2 * P * pair
-                nc.sync.dma_start(
-                    out=raw[:],
-                    in_=src[r0 : r0 + 2 * P, UNIT_K * kh : UNIT_K * (kh + 1)].rearrange("(a p) k -> p a k", p=P),
-                )
-                raw_tiles[(j, pair)] = raw
+        def load_while_room():
+            while state["loaded"] < len(blocks) and blocks[state["loaded"]][3] <= state["raw_free"]:
+                b = state["loaded"]
+                src, row0, g0, passes = blocks[b][:4]
+                k0 = PASS_K * g0
+                if passes == 1:
+                    raw = raw_pool.tile([P, 4, PASS_K], BF16, name="raw", tag="raw")
+                    raw_tiles[b] = [raw]
+                    for pair in range(2):
+                        r0 = row0 + 2 * P * pair
+                        nc.sync.dma_start(
+                            out=raw[:, 2 * pair : 2 * pair + 2, :],
+                            in_=src[r0 : r0 + 2 * P, k0 : k0 + PASS_K].rearrange("(a p) k -> p a k", p=P),
+                        )
+                else:
+                    raw_tiles[b] = []
+                    for pair in range(2):
+                        raw = raw_pool.tile([P, 2, 2 * PASS_K], BF16, name="raw", tag="raw")
+                        r0 = row0 + 2 * P * pair
+                        nc.sync.dma_start(
+                            out=raw[:],
+                            in_=src[r0 : r0 + 2 * P, k0 : k0 + 2 * PASS_K].rearrange("(a p) k -> p a k", p=P),
+                        )
+                        raw_tiles[b].append(raw)
+                state["raw_free"] -= passes
+                state["loaded"] += 1
 
-        for j in range(RAW_UNITS):
-            load(j)
+        def release_raw(b):
+            released.add(b)
+            while state["oldest"] in released:
+                state["raw_free"] += blocks[state["oldest"]][3]
+                state["oldest"] += 1
+            load_while_room()
+
+        load_while_room()
 
         zeros_bf16 = const.tile([P, 512], BF16, name="zeros_bf16")
         nc.vector.memset(zeros_bf16[:], 0.0)
@@ -106,8 +157,8 @@ def tile_virtual16bmatmul_kernel(tc, x, weight_upper, weight_lower, out_0, out_1
 
         idle_matmuls(WARM_UP)
 
-        x_codes = const.tile([P, 4, TOKENS], U32, name="x_codes", align_bytes=64)
-        x_scales = const.tile([P, 4, TOKENS], U8, name="x_scales", align_bytes=64)
+        x_codes = const.tile([P, PASSES, TOKENS], U32, name="x_codes", align_bytes=64)
+        x_scales = const.tile([P, PASSES, TOKENS], U8, name="x_scales", align_bytes=64)
         rows = []
         for i in range(TOKEN_TILES):
             row_tile = const.tile([P, N_OUT + MAX_SLOTS], F32, name="rows%d" % i)
@@ -116,58 +167,55 @@ def tile_virtual16bmatmul_kernel(tc, x, weight_upper, weight_lower, out_0, out_1
         row_inv = const.tile([P, TOKEN_TILES], F32, name="row_inv")
         row_factor = const.tile([P, TOKEN_TILES], F32, name="row_factor")
 
-        def split_words(j):
-            for pair in range(2):
-                split = split_pool.tile([P, 4, 2, P], F32, name="split", tag="split")
-                nc.vector.tensor_copy(
-                    out=split[:],
-                    in_=raw_tiles[(j, pair)][:]
-                    .rearrange("p a k -> p (a k)")
-                    .bitcast(F32)
-                    .rearrange("p (q m u) -> p q u m", q=4, u=2),
-                )
-                split_tiles[(j, pair)] = split
+        def split_up_to(last_item):
+            while state["split"] < len(blocks) and first_item[state["split"]] <= last_item:
+                b = state["split"]
+                split_tiles[b] = []
+                if b < DIRECT_BLOCKS:
+                    state["split"] += 1
+                    continue
+                for raw in raw_tiles[b]:
+                    split = split_pool.tile([P, 4, 2, P], F32, name="split", tag="split")
+                    nc.vector.tensor_copy(
+                        out=split[:],
+                        in_=raw[:].rearrange("p a k -> p (a k)").bitcast(F32).rearrange("p (q m u) -> p q u m", q=4, u=2),
+                    )
+                    split_tiles[b].append(split)
+                state["split"] += 1
+                release_raw(b)
 
-        def quantize(j, grouped, g):
-            nc.vector.quantize_mx(
-                out=codes[j][0][:, g, :].bitcast(FP8X4),
-                scales=codes[j][1][:, g, :],
-                in_=grouped[:, g, :, :].rearrange("p c t -> p (c t)"),
-            )
-
-        def transpose_and_quantize(j):
-            kh, n = units[j][2:4]
-            grouped = grouped_pool.tile([P, 2, CHUNK, 4], BF16, name="grouped", tag="grouped", align_bytes=64)
+        def transpose_and_quantize(t):
+            b, g = items[t]
+            g0, passes, n = blocks[b][2:]
+            grouped = grouped_pool.tile([P, CHUNK, 4], BF16, name="grouped", tag="grouped", align_bytes=64)
             grouped_words = grouped[:].bitcast(F32)
             if n < 0:
-                codes[j] = (x_codes[:, 2 * kh : 2 * kh + 2, :], x_scales[:, 2 * kh : 2 * kh + 2, :])
+                codes[t] = (x_codes[:, g0 + g, :], x_scales[:, g0 + g, :])
             else:
-                w_codes = code_pool.tile([P, 2, CHUNK], U32, name="w_codes", tag="w_codes", align_bytes=64)
-                w_scales = code_pool.tile([P, 2, CHUNK], U8, name="w_scales", tag="w_scales", align_bytes=64)
-                codes[j] = (w_codes[:], w_scales[:])
-            head = j < HEAD_UNITS
-            if head:
-                order = [(pair, g) for pair in range(2) for g in range(2)]
-            else:
-                order = [(pair, g) for g in range(2) for pair in range(2)]
-            for b, (pair, g) in enumerate(order):
+                w_codes = code_pool.tile([P, CHUNK], U32, name="w_codes", tag="w_codes", align_bytes=64)
+                w_scales = code_pool.tile([P, CHUNK], U8, name="w_scales", tag="w_scales", align_bytes=64)
+                codes[t] = (w_codes[:], w_scales[:])
+            for pair in range(2):
                 turned = psum.tile([P, 2, 2, P], F32, name="turned", tag="turned", bufs=TRANSPOSE_BANKS)
                 for a in range(2):
                     for u in range(2):
-                        nc.tensor.transpose(turned[:, a, u, :], split_tiles[(j, pair)][:, 2 * a + g, u, :], identity[:])
+                        if b < DIRECT_BLOCKS:
+                            first = 2 * P * (2 * pair + a)
+                            words = raw_tiles[b][0][:].rearrange("p a k -> p (a k)").bitcast(F32)[:, first + u : first + 2 * P : 2]
+                        elif passes == 1:
+                            words = split_tiles[b][0][:, 2 * pair + a, u, :]
+                        else:
+                            words = split_tiles[b][pair][:, 2 * a + g, u, :]
+                        nc.tensor.transpose(turned[:, a, u, :], words, identity[:])
                 nc.scalar.copy(
-                    out=grouped_words[:, g, 2 * P * pair : 2 * P * (pair + 1), :].rearrange("p (a r) u -> p a r u", a=2),
+                    out=grouped_words[:, 2 * P * pair : 2 * P * (pair + 1), :].rearrange("p (a r) u -> p a r u", a=2),
                     in_=turned[:].rearrange("p a u r -> p a r u"),
                 )
-                if head and b == 1:
-                    idle_matmuls(2)
-                if head and b == 3:
-                    idle_matmuls(1)
-                if not head and b == 1:
-                    quantize(j, grouped, 0)
-            if head:
-                quantize(j, grouped, 0)
-            quantize(j, grouped, 1)
+            nc.vector.quantize_mx(
+                out=codes[t][0].bitcast(FP8X4), scales=codes[t][1], in_=grouped[:].rearrange("p c t -> p (c t)")
+            )
+            if b < DIRECT_BLOCKS:
+                release_raw(b)
 
         def reduce_pending_maxima():
             for i, c0, width, slot in pending_maxima:
@@ -177,43 +225,50 @@ def tile_virtual16bmatmul_kernel(tc, x, weight_upper, weight_lower, out_0, out_1
                 )
             pending_maxima.clear()
 
+        def vector_share(i):
+            return VECTOR_CAST if i < TOKEN_TILES - 1 else VECTOR_CAST_LAST
+
         def scalar_cast_and_store(i):
+            first = vector_share(i)
             nc.scalar.activation(
-                out=byte_tiles[i][:, VECTOR_CAST:N_OUT], in_=rows[i][:, VECTOR_CAST:N_OUT], func=ACT.Identity,
+                out=byte_tiles[i][:, first:N_OUT], in_=rows[i][:, first:N_OUT], func=ACT.Identity,
                 bias=zero[:, 0:1], scale=row_factor[:, i : i + 1], saturate=False,
             )
-            nc.sync.dma_start(out=byte_rows[P * i : P * (i + 1), :], in_=byte_tiles[i][:].bitcast(U8))
+            nc.sync.dma_start(out=byte_rows[P * i : P * (i + 1), first:N_OUT], in_=byte_tiles[i][:, first:N_OUT].bitcast(U8))
 
-        def multiply(j, i, first_col, width):
-            kh, n, opens, closes = units[j][2:]
+        def multiply(t, i, first_col, width, opens, closes):
+            b, g = items[t]
+            g0, passes, n = blocks[b][2:]
             if opens:
                 bank = psum.tile([P, width], F32, name="bank", tag="sums", bufs=SUM_BANKS)
                 sums[i] = bank
-            for g in range(2):
-                nc.tensor.matmul_mx(
-                    out=sums[i][:],
-                    lhsT=x_codes[:, 2 * kh + g, P * i : P * (i + 1)].bitcast(FP8X4),
-                    lhsT_scale=x_scales[:, 2 * kh + g, P * i : P * (i + 1)],
-                    rhs=codes[j][0][:, g, first_col : first_col + width].bitcast(FP8X4),
-                    rhs_scale=codes[j][1][:, g, first_col : first_col + width],
-                    start=(opens and g == 0),
-                    stop=(closes and g == 1),
-                )
+            nc.tensor.matmul_mx(
+                out=sums[i][:],
+                lhsT=x_codes[:, g0 + g, P * i : P * (i + 1)].bitcast(FP8X4),
+                lhsT_scale=x_scales[:, g0 + g, P * i : P * (i + 1)],
+                rhs=codes[t][0][:, first_col : first_col + width].bitcast(FP8X4),
+                rhs_scale=codes[t][1][:, first_col : first_col + width],
+                start=opens,
+                stop=closes,
+            )
             if not closes:
                 return
             c0 = CHUNK * n + first_col
             nc.scalar.copy(out=rows[i][:, c0 : c0 + width], in_=sums[i][:])
             nc.sync.dma_start(out=out_rows[P * i : P * (i + 1), c0 : c0 + width], in_=rows[i][:, c0 : c0 + width])
+            for waiting in waiting_casts:
+                scalar_cast_and_store(waiting)
+            waiting_casts.clear()
+            deferred = DEFER_MAX and i < LEAD_TILES
             if c0 + width < N_OUT:
-                pending_maxima.append((i, c0, width, maxima_kept[i]))
-                maxima_kept[i] += 1
+                if not deferred:
+                    pending_maxima.append((i, c0, width, maxima_kept[i]))
+                    maxima_kept[i] += 1
                 return
-            if i > 0:
-                scalar_cast_and_store(i - 1)
             reduce_pending_maxima()
             nc.vector.tensor_reduce(
-                out=row_max[:, i : i + 1], in_=rows[i][:, c0 : N_OUT + maxima_kept[i]], axis=AX.X, op=ALU.max,
-                apply_absolute_value=True,
+                out=row_max[:, i : i + 1], in_=rows[i][:, (0 if deferred else c0) : N_OUT + maxima_kept[i]], axis=AX.X,
+                op=ALU.max, apply_absolute_value=True,
             )
             nc.vector.reciprocal(out=row_inv[:, i : i + 1], in_=row_max[:, i : i + 1])
             nc.vector.tensor_scalar(
@@ -221,25 +276,41 @@ def tile_virtual16bmatmul_kernel(tc, x, weight_upper, weight_lower, out_0, out_1
             )
             as_bytes = byte_pool.tile([P, N_OUT], FP8, name="as_bytes", tag="as_bytes")
             byte_tiles[i] = as_bytes
+            share = vector_share(i)
             nc.vector.tensor_scalar(
-                out=as_bytes[:, 0:VECTOR_CAST], in0=rows[i][:, 0:VECTOR_CAST], scalar1=row_factor[:, i : i + 1],
+                out=as_bytes[:, 0:share], in0=rows[i][:, 0:share], scalar1=row_factor[:, i : i + 1],
                 scalar2=None, op0=ALU.mult, saturate=False,
             )
+            nc.sync.dma_start(out=byte_rows[P * i : P * (i + 1), 0:share], in_=as_bytes[:, 0:share].bitcast(U8))
+            waiting_casts.append(i)
 
-        done = 0
-        split_words(0)
-        for j in range(len(units)):
-            if j + 1 < len(units):
-                split_words(j + 1)
+        if SPLIT_AFTER:
+            split_up_to(SPLIT_LEAD)
+        for r, run in enumerate(runs):
+            if not SPLIT_AFTER:
+                split_up_to(run[-1] + SPLIT_LEAD)
             reduce_pending_maxima()
-            transpose_and_quantize(j)
-            if j + RAW_UNITS < len(units):
-                load(j + RAW_UNITS)
-            for s in range(STEPS_PER_RUN):
-                if steps[done][0] < j:
-                    multiply(*steps[done])
-                    done += 1
-        for step in steps[done:]:
+            for t in run:
+                transpose_and_quantize(t)
+                if steps[0][0] > run[0] - LAG:
+                    idle_matmuls(HEAD_IDLE)
+            if SPLIT_AFTER:
+                split_up_to(run[-1] + 1 + SPLIT_LEAD)
+            state["credit"] = min(state["credit"], CARRY) + (P_SMALL if len(run) == 1 else P_BIG)
+            closed_before = state["closed"]
+            while state["credit"] > 0:
+                step = steps[state["done"]]
+                if step[0] > run[0] - LAG:
+                    break
+                if step[4] and state["opened"] - SUM_BANKS >= closed_before:
+                    break
+                multiply(*step)
+                state["done"] += 1
+                state["credit"] -= 1
+                state["opened"] += 1 if step[4] else 0
+                state["closed"] += 1 if step[5] else 0
+        for step in steps[state["done"] :]:
             multiply(*step)
             reduce_pending_maxima()
-        scalar_cast_and_store(TOKEN_TILES - 1)
+        for waiting in waiting_casts:
+            scalar_cast_and_store(waiting)

@@ -31,9 +31,11 @@ SUM_BANKS = 8 - TRANSPOSE_BANKS
 LEAD_TILES = 3
 STAGGER = 0
 DEFER_MAX = 0
-WARM_UP = 7
-HEAD_IDLE = 1
-DIRECT_BLOCKS = 0
+WARM_UP = 5
+HEAD_IDLE = 0
+DIRECT_BLOCKS = 3
+VECTOR_EMPTIES = 2
+VECTOR_BANKS = (3,)
 SPLIT_LEAD = 2
 SPLIT_AFTER = 0
 LAG = 2
@@ -199,7 +201,10 @@ def tile_virtual16bmatmul_kernel(tc, x, weight_upper, weight_lower, out_0, out_1
                 turned = psum.tile([P, 2, 2, P], F32, name="turned", tag="turned", bufs=TRANSPOSE_BANKS)
                 for a in range(2):
                     for u in range(2):
-                        if b < DIRECT_BLOCKS:
+                        if b < DIRECT_BLOCKS and passes == 2:
+                            first = 2 * P * (2 * a + g)
+                            words = raw_tiles[b][pair][:].rearrange("p a k -> p (a k)").bitcast(F32)[:, first + u : first + 2 * P : 2]
+                        elif b < DIRECT_BLOCKS:
                             first = 2 * P * (2 * pair + a)
                             words = raw_tiles[b][0][:].rearrange("p a k -> p (a k)").bitcast(F32)[:, first + u : first + 2 * P : 2]
                         elif passes == 1:
@@ -207,14 +212,20 @@ def tile_virtual16bmatmul_kernel(tc, x, weight_upper, weight_lower, out_0, out_1
                         else:
                             words = split_tiles[b][pair][:, 2 * a + g, u, :]
                         nc.tensor.transpose(turned[:, a, u, :], words, identity[:])
-                nc.scalar.copy(
-                    out=grouped_words[:, 2 * P * pair : 2 * P * (pair + 1), :].rearrange("p (a r) u -> p a r u", a=2),
-                    in_=turned[:].rearrange("p a u r -> p a r u"),
-                )
+                if b < VECTOR_EMPTIES and (2 * g + pair) in VECTOR_BANKS:
+                    nc.vector.tensor_copy(
+                        out=grouped_words[:, 2 * P * pair : 2 * P * (pair + 1), :].rearrange("p (a r) u -> p a r u", a=2),
+                        in_=turned[:].rearrange("p a u r -> p a r u"),
+                    )
+                else:
+                    nc.scalar.copy(
+                        out=grouped_words[:, 2 * P * pair : 2 * P * (pair + 1), :].rearrange("p (a r) u -> p a r u", a=2),
+                        in_=turned[:].rearrange("p a u r -> p a r u"),
+                    )
             nc.vector.quantize_mx(
                 out=codes[t][0].bitcast(FP8X4), scales=codes[t][1], in_=grouped[:].rearrange("p c t -> p (c t)")
             )
-            if b < DIRECT_BLOCKS:
+            if b < DIRECT_BLOCKS and g == passes - 1:
                 release_raw(b)
 
         def reduce_pending_maxima():

@@ -45,7 +45,9 @@ CARRY = 100
 LAST_PIECES = (256, 128, 128)
 MAX_SLOTS = 8
 VECTOR_CAST = 1024
-VECTOR_CAST_LAST = 1024
+VECTOR_CAST_LAST = 1408
+SHORT_CHAIN = 1
+CAST_PIECES = 2
 
 
 def tile_virtual16bmatmul_kernel(tc, x, weight_upper, weight_lower, out_0, out_1):
@@ -168,6 +170,7 @@ def tile_virtual16bmatmul_kernel(tc, x, weight_upper, weight_lower, out_0, out_1
         row_max = const.tile([P, TOKEN_TILES], F32, name="row_max")
         row_inv = const.tile([P, TOKEN_TILES], F32, name="row_inv")
         row_factor = const.tile([P, TOKEN_TILES], F32, name="row_factor")
+        scaled = const.tile([P, P + MAX_SLOTS], F32, name="scaled")
 
         def split_up_to(last_item):
             while state["split"] < len(blocks) and first_item[state["split"]] <= last_item:
@@ -241,11 +244,15 @@ def tile_virtual16bmatmul_kernel(tc, x, weight_upper, weight_lower, out_0, out_1
 
         def scalar_cast_and_store(i):
             first = vector_share(i)
-            nc.scalar.activation(
-                out=byte_tiles[i][:, first:N_OUT], in_=rows[i][:, first:N_OUT], func=ACT.Identity,
-                bias=zero[:, 0:1], scale=row_factor[:, i : i + 1], saturate=False,
-            )
-            nc.sync.dma_start(out=byte_rows[P * i : P * (i + 1), first:N_OUT], in_=byte_tiles[i][:, first:N_OUT].bitcast(U8))
+            pieces = CAST_PIECES if i == TOKEN_TILES - 1 else 1
+            for piece in range(pieces):
+                b0 = first + (N_OUT - first) * piece // pieces
+                b1 = first + (N_OUT - first) * (piece + 1) // pieces
+                nc.scalar.activation(
+                    out=byte_tiles[i][:, b0:b1], in_=rows[i][:, b0:b1], func=ACT.Identity,
+                    bias=zero[:, 0:1], scale=row_factor[:, i : i + 1], saturate=False,
+                )
+                nc.sync.dma_start(out=byte_rows[P * i : P * (i + 1), b0:b1], in_=byte_tiles[i][:, b0:b1].bitcast(U8))
 
         def multiply(t, i, first_col, width, opens, closes):
             b, g = items[t]
@@ -265,6 +272,9 @@ def tile_virtual16bmatmul_kernel(tc, x, weight_upper, weight_lower, out_0, out_1
             if not closes:
                 return
             c0 = CHUNK * n + first_col
+            short_chain = SHORT_CHAIN and i == TOKEN_TILES - 1 and c0 + width == N_OUT
+            if short_chain:
+                nc.scalar.activation(out=scaled[:, 0:width], in_=sums[i][:], func=ACT.Copy, scale=1.0 / 448.0)
             nc.scalar.copy(out=rows[i][:, c0 : c0 + width], in_=sums[i][:])
             nc.sync.dma_start(out=out_rows[P * i : P * (i + 1), c0 : c0 + width], in_=rows[i][:, c0 : c0 + width])
             for waiting in waiting_casts:
@@ -277,22 +287,37 @@ def tile_virtual16bmatmul_kernel(tc, x, weight_upper, weight_lower, out_0, out_1
                     maxima_kept[i] += 1
                 return
             reduce_pending_maxima()
-            nc.vector.tensor_reduce(
-                out=row_max[:, i : i + 1], in_=rows[i][:, (0 if deferred else c0) : N_OUT + maxima_kept[i]], axis=AX.X,
-                op=ALU.max, apply_absolute_value=True,
-            )
-            nc.vector.reciprocal(out=row_inv[:, i : i + 1], in_=row_max[:, i : i + 1])
-            nc.vector.tensor_scalar(
-                out=row_factor[:, i : i + 1], in0=row_inv[:, i : i + 1], scalar1=448.0, scalar2=None, op0=ALU.mult
-            )
+            if short_chain:
+                nc.vector.tensor_scalar(
+                    out=scaled[:, width : width + maxima_kept[i]], in0=rows[i][:, N_OUT : N_OUT + maxima_kept[i]],
+                    scalar1=1.0 / 448.0, scalar2=None, op0=ALU.mult,
+                )
+                nc.vector.tensor_reduce(
+                    out=row_max[:, i : i + 1], in_=scaled[:, 0 : width + maxima_kept[i]], axis=AX.X, op=ALU.max,
+                    apply_absolute_value=True,
+                )
+                nc.vector.reciprocal(out=row_factor[:, i : i + 1], in_=row_max[:, i : i + 1])
+            else:
+                nc.vector.tensor_reduce(
+                    out=row_max[:, i : i + 1], in_=rows[i][:, (0 if deferred else c0) : N_OUT + maxima_kept[i]], axis=AX.X,
+                    op=ALU.max, apply_absolute_value=True,
+                )
+                nc.vector.reciprocal(out=row_inv[:, i : i + 1], in_=row_max[:, i : i + 1])
+                nc.vector.tensor_scalar(
+                    out=row_factor[:, i : i + 1], in0=row_inv[:, i : i + 1], scalar1=448.0, scalar2=None, op0=ALU.mult
+                )
             as_bytes = byte_pool.tile([P, N_OUT], FP8, name="as_bytes", tag="as_bytes")
             byte_tiles[i] = as_bytes
             share = vector_share(i)
-            nc.vector.tensor_scalar(
-                out=as_bytes[:, 0:share], in0=rows[i][:, 0:share], scalar1=row_factor[:, i : i + 1],
-                scalar2=None, op0=ALU.mult, saturate=False,
-            )
-            nc.sync.dma_start(out=byte_rows[P * i : P * (i + 1), 0:share], in_=as_bytes[:, 0:share].bitcast(U8))
+            pieces = CAST_PIECES if i == TOKEN_TILES - 1 else 1
+            for piece in range(pieces):
+                b0 = share * piece // pieces
+                b1 = share * (piece + 1) // pieces
+                nc.vector.tensor_scalar(
+                    out=as_bytes[:, b0:b1], in0=rows[i][:, b0:b1], scalar1=row_factor[:, i : i + 1],
+                    scalar2=None, op0=ALU.mult, saturate=False,
+                )
+                nc.sync.dma_start(out=byte_rows[P * i : P * (i + 1), b0:b1], in_=as_bytes[:, b0:b1].bitcast(U8))
             waiting_casts.append(i)
 
         if SPLIT_AFTER:

from contextlib import ExitStack

import concourse.mybir as mybir
from concourse.masks import make_identity

F32 = mybir.dt.float32
BF16 = mybir.dt.bfloat16
U32 = mybir.dt.uint32
U8 = mybir.dt.uint8
FP8X4 = mybir.dt.float8_e4m3fn_x4
FP8 = mybir.dt.float8_e4m3fn
ALU = mybir.AluOpType
ACT = mybir.ActivationFunctionType
AX = mybir.AxisListType

P = 128
TOKENS = 512
K = 2048
N_OUT = 2048
FLOPS = 2 * 2 * TOKENS * K * N_OUT

TOKEN_TILES = TOKENS // P
CHUNK = 512
CHUNKS = N_OUT // CHUNK
PASS_K = 512
PASSES = K // PASS_K
RAW_TILES = 12
SMALL_PASSES = 0
TRANSPOSE_BANKS = 4
SUM_BANKS = 8 - TRANSPOSE_BANKS
LEAD_TILES = 3
STAGGER = 0
DEFER_MAX = 0
WARM_UP = 5
HEAD_IDLE = 0
DIRECT_BLOCKS = 3
VECTOR_EMPTIES = 2
VECTOR_BANKS = (3,)
SPLIT_LEAD = 2
SPLIT_AFTER = 0
LAG = 2
P_SMALL = 3
P_BIG = 6
CARRY = 100
LAST_PIECES = (256, 128, 128)
MAX_SLOTS = 8
VECTOR_CAST = 1024
VECTOR_CAST_LAST = 1408
SHORT_CHAIN = 1
CAST_PIECES = 2


def tile_virtual16bmatmul_kernel(tc, x, weight_upper, weight_lower, out_0, out_1):
    nc = tc.nc
    x_rows = x.flatten_outer_dims()
    out_rows = out_0.flatten_outer_dims()
    byte_rows = out_1.flatten_outer_dims()

    blocks = []
    for g in range(SMALL_PASSES):
        blocks.append((x_rows, 0, g, 1, -1))
        blocks.append((weight_upper, 0, g, 1, 0))
        blocks.append((weight_lower, 0, g, 1, 0))
    for g in range(SMALL_PASSES, PASSES, 2):
        blocks.append((x_rows, 0, g, 2, -1))
        blocks.append((weight_upper, 0, g, 2, 0))
        blocks.append((weight_lower, 0, g, 2, 0))
    for n in range(1, CHUNKS):
        for g in range(0, PASSES, 2):
            blocks.append((weight_upper, CHUNK * n, g, 2, n))
            blocks.append((weight_lower, CHUNK * n, g, 2, n))

    items = [(b, g) for b in range(len(blocks)) for g in range(blocks[b][3])]
    first_item = [items.index((b, 0)) for b in range(len(blocks))]
    runs = [[t for t in range(len(items)) if items[t][0] == b] for b in range(len(blocks))]

    w_items = [t for t in range(len(items)) if blocks[items[t][0]][4] >= 0]
    per_chunk = len(w_items) // CHUNKS
    order = []
    for v in range(len(w_items) + STAGGER * (LEAD_TILES - 1)):
        for i in range(LEAD_TILES):
            w = v - STAGGER * i
            if 0 <= w < len(w_items):
                order.append((w, i, 0, CHUNK))
    for i in range(LEAD_TILES, TOKEN_TILES):
        order.extend((w, i, 0, CHUNK) for w in range(len(w_items) - per_chunk))
        for piece, width in enumerate(LAST_PIECES):
            order.extend((w, i, sum(LAST_PIECES[:piece]), width) for w in range(len(w_items) - per_chunk, len(w_items)))
    steps = [(w_items[w], i, c, width, w % per_chunk == 0, w % per_chunk == per_chunk - 1) for w, i, c, width in order]

    with ExitStack() as ctx:
        const = ctx.enter_context(tc.tile_pool(name="const", bufs=1))
        raw_pool = ctx.enter_context(tc.tile_pool(name="raw_pool", bufs=RAW_TILES))
        split_pool = ctx.enter_context(tc.tile_pool(name="split_pool", bufs=6))
        grouped_pool = ctx.enter_context(tc.tile_pool(name="grouped_pool", bufs=6))
        code_pool = ctx.enter_context(tc.tile_pool(name="code_pool", bufs=32))
        byte_pool = ctx.enter_context(tc.tile_pool(name="byte_pool", bufs=TOKEN_TILES))
        psum = ctx.enter_context(tc.psum_pool(name="psum", bufs=1))
        ctx.enter_context(tc.manual_schedule())

        raw_tiles = {}
        split_tiles = {}
        codes = {}
        sums = {}
        byte_tiles = {}
        released = set()
        waiting_casts = []
        pending_maxima = []
        maxima_kept = [0] * TOKEN_TILES
        state = {"loaded": 0, "raw_free": RAW_TILES, "split": 0, "oldest": 0, "done": 0, "credit": 0, "opened": 0, "closed": 0}

        def load_while_room():
            while state["loaded"] < len(blocks) and blocks[state["loaded"]][3] <= state["raw_free"]:
                b = state["loaded"]
                src, row0, g0, passes = blocks[b][:4]
                k0 = PASS_K * g0
                if passes == 1:
                    raw = raw_pool.tile([P, 4, PASS_K], BF16, name="raw", tag="raw")
                    raw_tiles[b] = [raw]
                    for pair in range(2):
                        r0 = row0 + 2 * P * pair
                        nc.sync.dma_start(
                            out=raw[:, 2 * pair : 2 * pair + 2, :],
                            in_=src[r0 : r0 + 2 * P, k0 : k0 + PASS_K].rearrange("(a p) k -> p a k", p=P),
                        )
                else:
                    raw_tiles[b] = []
                    for pair in range(2):
                        raw = raw_pool.tile([P, 2, 2 * PASS_K], BF16, name="raw", tag="raw")
                        r0 = row0 + 2 * P * pair
                        nc.sync.dma_start(
                            out=raw[:],
                            in_=src[r0 : r0 + 2 * P, k0 : k0 + 2 * PASS_K].rearrange("(a p) k -> p a k", p=P),
                        )
                        raw_tiles[b].append(raw)
                state["raw_free"] -= passes
                state["loaded"] += 1

        def release_raw(b):
            released.add(b)
            while state["oldest"] in released:
                state["raw_free"] += blocks[state["oldest"]][3]
                state["oldest"] += 1
            load_while_room()

        load_while_room()

        zeros_bf16 = const.tile([P, 512], BF16, name="zeros_bf16")
        nc.vector.memset(zeros_bf16[:], 0.0)
        identity = const.tile([P, P], F32, name="identity")
        make_identity(nc, identity[:])
        zero = const.tile([P, 1], F32, name="zero")
        nc.vector.memset(zero[:], 0.0)
        scratch = const.tile([P, 1], F32, name="scratch")
        nc.scalar.activation(out=scratch[:], in_=zero[:], func=ACT.Identity, bias=zero[:, 0:1], scale=zero[:, 0:1])

        def idle_matmuls(count):
            for d in range(count):
                unused = psum.tile([P, 512], F32, name="unused", tag="sums", bufs=SUM_BANKS)
                nc.tensor.matmul(out=unused[:], lhsT=zeros_bf16[:, 0:P], rhs=zeros_bf16[:], start=True, stop=True)

        idle_matmuls(WARM_UP)

        x_codes = const.tile([P, PASSES, TOKENS], U32, name="x_codes", align_bytes=64)
        x_scales = const.tile([P, PASSES, TOKENS], U8, name="x_scales", align_bytes=64)
        rows = []
        for i in range(TOKEN_TILES):
            row_tile = const.tile([P, N_OUT + MAX_SLOTS], F32, name="rows%d" % i)
            rows.append(row_tile)
        row_max = const.tile([P, TOKEN_TILES], F32, name="row_max")
        row_inv = const.tile([P, TOKEN_TILES], F32, name="row_inv")
        row_factor = const.tile([P, TOKEN_TILES], F32, name="row_factor")
        scaled = const.tile([P, P + MAX_SLOTS], F32, name="scaled")

        def split_up_to(last_item):
            while state["split"] < len(blocks) and first_item[state["split"]] <= last_item:
                b = state["split"]
                split_tiles[b] = []
                if b < DIRECT_BLOCKS:
                    state["split"] += 1
                    continue
                for raw in raw_tiles[b]:
                    split = split_pool.tile([P, 4, 2, P], F32, name="split", tag="split")
                    nc.vector.tensor_copy(
                        out=split[:],
                        in_=raw[:].rearrange("p a k -> p (a k)").bitcast(F32).rearrange("p (q m u) -> p q u m", q=4, u=2),
                    )
                    split_tiles[b].append(split)
                state["split"] += 1
                release_raw(b)

        def transpose_and_quantize(t):
            b, g = items[t]
            g0, passes, n = blocks[b][2:]
            grouped = grouped_pool.tile([P, CHUNK, 4], BF16, name="grouped", tag="grouped", align_bytes=64)
            grouped_words = grouped[:].bitcast(F32)
            if n < 0:
                codes[t] = (x_codes[:, g0 + g, :], x_scales[:, g0 + g, :])
            else:
                w_codes = code_pool.tile([P, CHUNK], U32, name="w_codes", tag="w_codes", align_bytes=64)
                w_scales = code_pool.tile([P, CHUNK], U8, name="w_scales", tag="w_scales", align_bytes=64)
                codes[t] = (w_codes[:], w_scales[:])
            for pair in range(2):
                turned = psum.tile([P, 2, 2, P], F32, name="turned", tag="turned", bufs=TRANSPOSE_BANKS)
                for a in range(2):
                    for u in range(2):
                        if b < DIRECT_BLOCKS and passes == 2:
                            first = 2 * P * (2 * a + g)
                            words = raw_tiles[b][pair][:].rearrange("p a k -> p (a k)").bitcast(F32)[:, first + u : first + 2 * P : 2]
                        elif b < DIRECT_BLOCKS:
                            first = 2 * P * (2 * pair + a)
                            words = raw_tiles[b][0][:].rearrange("p a k -> p (a k)").bitcast(F32)[:, first + u : first + 2 * P : 2]
                        elif passes == 1:
                            words = split_tiles[b][0][:, 2 * pair + a, u, :]
                        else:
                            words = split_tiles[b][pair][:, 2 * a + g, u, :]
                        nc.tensor.transpose(turned[:, a, u, :], words, identity[:])
                if b < VECTOR_EMPTIES and (2 * g + pair) in VECTOR_BANKS:
                    nc.vector.tensor_copy(
                        out=grouped_words[:, 2 * P * pair : 2 * P * (pair + 1), :].rearrange("p (a r) u -> p a r u", a=2),
                        in_=turned[:].rearrange("p a u r -> p a r u"),
                    )
                else:
                    nc.scalar.copy(
                        out=grouped_words[:, 2 * P * pair : 2 * P * (pair + 1), :].rearrange("p (a r) u -> p a r u", a=2),
                        in_=turned[:].rearrange("p a u r -> p a r u"),
                    )
            nc.vector.quantize_mx(
                out=codes[t][0].bitcast(FP8X4), scales=codes[t][1], in_=grouped[:].rearrange("p c t -> p (c t)")
            )
            if b < DIRECT_BLOCKS and g == passes - 1:
                release_raw(b)

        def reduce_pending_maxima():
            for i, c0, width, slot in pending_maxima:
                nc.vector.tensor_reduce(
                    out=rows[i][:, N_OUT + slot : N_OUT + slot + 1], in_=rows[i][:, c0 : c0 + width], axis=AX.X,
                    op=ALU.max, apply_absolute_value=True,
                )
            pending_maxima.clear()

        def vector_share(i):
            return VECTOR_CAST if i < TOKEN_TILES - 1 else VECTOR_CAST_LAST

        def scalar_cast_and_store(i):
            first = vector_share(i)
            pieces = CAST_PIECES if i == TOKEN_TILES - 1 else 1
            for piece in range(pieces):
                b0 = first + (N_OUT - first) * piece // pieces
                b1 = first + (N_OUT - first) * (piece + 1) // pieces
                nc.scalar.activation(
                    out=byte_tiles[i][:, b0:b1], in_=rows[i][:, b0:b1], func=ACT.Identity,
                    bias=zero[:, 0:1], scale=row_factor[:, i : i + 1], saturate=False,
                )
                nc.sync.dma_start(out=byte_rows[P * i : P * (i + 1), b0:b1], in_=byte_tiles[i][:, b0:b1].bitcast(U8))

        def multiply(t, i, first_col, width, opens, closes):
            b, g = items[t]
            g0, passes, n = blocks[b][2:]
            if opens:
                bank = psum.tile([P, width], F32, name="bank", tag="sums", bufs=SUM_BANKS)
                sums[i] = bank
            nc.tensor.matmul_mx(
                out=sums[i][:],
                lhsT=x_codes[:, g0 + g, P * i : P * (i + 1)].bitcast(FP8X4),
                lhsT_scale=x_scales[:, g0 + g, P * i : P * (i + 1)],
                rhs=codes[t][0][:, first_col : first_col + width].bitcast(FP8X4),
                rhs_scale=codes[t][1][:, first_col : first_col + width],
                start=opens,
                stop=closes,
            )
            if not closes:
                return
            c0 = CHUNK * n + first_col
            short_chain = SHORT_CHAIN and i == TOKEN_TILES - 1 and c0 + width == N_OUT
            if short_chain:
                nc.scalar.activation(out=scaled[:, 0:width], in_=sums[i][:], func=ACT.Copy, scale=1.0 / 448.0)
            nc.scalar.copy(out=rows[i][:, c0 : c0 + width], in_=sums[i][:])
            nc.sync.dma_start(out=out_rows[P * i : P * (i + 1), c0 : c0 + width], in_=rows[i][:, c0 : c0 + width])
            for waiting in waiting_casts:
                scalar_cast_and_store(waiting)
            waiting_casts.clear()
            deferred = DEFER_MAX and i < LEAD_TILES
            if c0 + width < N_OUT:
                if not deferred:
                    pending_maxima.append((i, c0, width, maxima_kept[i]))
                    maxima_kept[i] += 1
                return
            reduce_pending_maxima()
            if short_chain:
                nc.vector.tensor_scalar(
                    out=scaled[:, width : width + maxima_kept[i]], in0=rows[i][:, N_OUT : N_OUT + maxima_kept[i]],
                    scalar1=1.0 / 448.0, scalar2=None, op0=ALU.mult,
                )
                nc.vector.tensor_reduce(
                    out=row_max[:, i : i + 1], in_=scaled[:, 0 : width + maxima_kept[i]], axis=AX.X, op=ALU.max,
                    apply_absolute_value=True,
                )
                nc.vector.reciprocal(out=row_factor[:, i : i + 1], in_=row_max[:, i : i + 1])
            else:
                nc.vector.tensor_reduce(
                    out=row_max[:, i : i + 1], in_=rows[i][:, (0 if deferred else c0) : N_OUT + maxima_kept[i]], axis=AX.X,
                    op=ALU.max, apply_absolute_value=True,
                )
                nc.vector.reciprocal(out=row_inv[:, i : i + 1], in_=row_max[:, i : i + 1])
                nc.vector.tensor_scalar(
                    out=row_factor[:, i : i + 1], in0=row_inv[:, i : i + 1], scalar1=448.0, scalar2=None, op0=ALU.mult
                )
            as_bytes = byte_pool.tile([P, N_OUT], FP8, name="as_bytes", tag="as_bytes")
            byte_tiles[i] = as_bytes
            share = vector_share(i)
            pieces = CAST_PIECES if i == TOKEN_TILES - 1 else 1
            for piece in range(pieces):
                b0 = share * piece // pieces
                b1 = share * (piece + 1) // pieces
                nc.vector.tensor_scalar(
                    out=as_bytes[:, b0:b1], in0=rows[i][:, b0:b1], scalar1=row_factor[:, i : i + 1],
                    scalar2=None, op0=ALU.mult, saturate=False,
                )
                nc.sync.dma_start(out=byte_rows[P * i : P * (i + 1), b0:b1], in_=as_bytes[:, b0:b1].bitcast(U8))
            waiting_casts.append(i)

        if SPLIT_AFTER:
            split_up_to(SPLIT_LEAD)
        for r, run in enumerate(runs):
            if not SPLIT_AFTER:
                split_up_to(run[-1] + SPLIT_LEAD)
            reduce_pending_maxima()
            for t in run:
                transpose_and_quantize(t)
                if steps[0][0] > run[0] - LAG:
                    idle_matmuls(HEAD_IDLE)
            if SPLIT_AFTER:
                split_up_to(run[-1] + 1 + SPLIT_LEAD)
            state["credit"] = min(state["credit"], CARRY) + (P_SMALL if len(run) == 1 else P_BIG)
            closed_before = state["closed"]
            while state["credit"] > 0:
                step = steps[state["done"]]
                if step[0] > run[0] - LAG:
                    break
                if step[4] and state["opened"] - SUM_BANKS >= closed_before:
                    break
                multiply(*step)
                state["done"] += 1
                state["credit"] -= 1
                state["opened"] += 1 if step[4] else 0
                state["closed"] += 1 if step[5] else 0
        for step in steps[state["done"] :]:
            multiply(*step)
            reduce_pending_maxima()
        for waiting in waiting_casts:
            scalar_cast_and_store(waiting)
